import numpy as np
import ml_dtypes


def mxq(x, axis, fmt="e4m3"):
    dtype, down = {"e4m3": (ml_dtypes.float8_e4m3fn, 7), "e5m2": (ml_dtypes.float8_e5m2, 14)}[fmt]
    v = np.moveaxis(np.asarray(x, np.float32).astype(ml_dtypes.bfloat16).astype(np.float64), axis, -1)
    blocks = v.reshape(v.shape[:-1] + (-1, 32))
    amax = np.abs(blocks).max(-1, keepdims=True)
    byte = np.maximum(np.where(amax > 0, np.frexp(amax)[1] - 1 + 127, 0) - down, 1)
    scale = np.exp2(byte - 127.0)
    codes = (blocks / scale).astype(np.float32).astype(dtype).astype(np.float64)
    return np.moveaxis((codes * scale).reshape(v.shape), -1, axis)


WIDE = False


def mx_kscale(k):
    if not WIDE:
        return np.ones(k)
    levels = np.array([10, -10, 5, -5, 0])
    a = np.random.permutation(np.resize(levels, k // 512 * 4)).reshape(k // 512, 4)
    idx = np.arange(k)
    return np.exp2(a[idx // 512, idx % 128 // 32])


BF16 = ml_dtypes.bfloat16


def bf(x):
    return np.asarray(x, np.float32).astype(BF16)


def f64(x):
    return np.asarray(x).astype(np.float64)


E2M1 = np.array([0.0, 0.5, 1.0, 1.5, 2.0, 3.0, 4.0, 6.0, -0.0, -0.5, -1.0, -1.5, -2.0, -3.0, -4.0, -6.0])


def pack_weight(w, fmt):
    k, n = w.shape
    w = f64(bf(w)).reshape(k // 32, 32, n)
    amax = np.abs(w).max(1)
    if fmt == "e4m3":
        byte = np.frexp(amax)[1] - 1 + 127 - 7
    else:
        mant, ex = np.frexp(amax / 6.0)
        byte = np.where(mant > 0.5, ex, ex - 1) + 127
    byte = np.clip(np.where(amax > 0, byte, 1), 1, 254)
    scaled = (w * np.exp2(127.0 - byte)[:, None, :]).reshape(k, n).astype(np.float32)
    by_word = np.ascontiguousarray(scaled.reshape(k // 512, 128, 4, n).transpose(0, 1, 3, 2))
    if fmt == "e4m3":
        words = by_word.astype(ml_dtypes.float8_e4m3fn).view(np.uint8)
    else:
        c = by_word.astype(ml_dtypes.float4_e2m1fn).view(np.uint8) & 0xF
        words = c[..., 0::2] | (c[..., 1::2] << 4)
    return np.ascontiguousarray(words), np.ascontiguousarray(byte.astype(np.uint8).reshape(k // 512, 16, n))


def unpack_weight(words, scales, fmt):
    g, p, n, _ = words.shape
    if fmt == "e4m3":
        vals = np.ascontiguousarray(words).view(ml_dtypes.float8_e4m3fn).astype(np.float64)
    else:
        nib = np.empty((g, p, n, 4), np.uint8)
        nib[..., 0::2] = words & 0xF
        nib[..., 1::2] = words >> 4
        vals = E2M1[nib]
    vals = vals * np.repeat(np.exp2(scales.astype(np.float64) - 127.0), 8, axis=1)[..., None]
    return vals.transpose(0, 1, 3, 2).reshape(g * 512, n)

def pack4(w):
    words, scales = pack_weight(w, "e2m1")
    return words.reshape(words.shape[0], 128, -1), scales


def unpack4(words, scales):
    return unpack_weight(words.reshape(words.shape[0], 128, -1, 2), scales, "e2m1")


B, T, D, DH, H, W = 1, 128, 16384, 256, 4, 512
ROPE_BASE = 10000.0
EPS = 1.1920929e-07


def rope(u):
    freqs = ROPE_BASE ** (-2.0 * np.arange(DH // 2) / DH)
    theta = np.arange(T)[:, None] * freqs[None, :]
    cos, sin = np.cos(theta), np.sin(theta)
    u1, u2 = u[..., 0::2], u[..., 1::2]
    return np.stack([u1 * cos - u2 * sin, u1 * sin + u2 * cos], axis=-1).reshape(u.shape)


def rmsnorm(u, w):
    return u * (1.0 / np.sqrt(np.mean(u * u, axis=-1, keepdims=True) + EPS)) * w


def setup_inputs():
    s = mx_kscale(D)
    x = bf(np.random.standard_normal((B, T, D)) * s)
    wq = np.random.standard_normal((H * DH, D)) / np.sqrt(D) / s
    wkv = np.random.standard_normal((2 * DH, D)) * 2.0 / np.sqrt(D) / s
    q_norm_w = bf(1.0 + 0.1 * np.random.standard_normal(DH))
    k_norm_w = bf(1.0 + 0.1 * np.random.standard_normal(DH))
    wq_words, wq_scales = pack4(np.ascontiguousarray(wq.T))
    wkv_words, wkv_scales = pack4(np.ascontiguousarray(wkv.T))
    return {"x": x,
            "wq_words": wq_words, "wq_scales": wq_scales,
            "wkv_words": wkv_words, "wkv_scales": wkv_scales,
            "q_norm_w": q_norm_w,
            "k_norm_w": k_norm_w}


def reference(x, wq_words, wq_scales, wkv_words, wkv_scales, q_norm_w, k_norm_w):
    xq = mxq(f64(x), 2, "e4m3")
    q = xq @ unpack4(wq_words, wq_scales)
    kv = xq @ unpack4(wkv_words, wkv_scales)
    k, v = kv[..., :DH], kv[..., DH:]
    q = q.reshape(B, T, H, DH).transpose(0, 2, 1, 3)
    q_rot = rmsnorm(rope(q), f64(q_norm_w))
    k_rot = rmsnorm(rope(k), f64(k_norm_w))
    return q_rot, k_rot, v

@@ -1,0 +1,288 @@
+import math
+from contextlib import ExitStack
+
+import concourse.mybir as mybir
+from concourse.masks import make_identity
+
+F32 = mybir.dt.float32
+BF16 = mybir.dt.bfloat16
+I32 = mybir.dt.int32
+U32 = mybir.dt.uint32
+U8 = mybir.dt.uint8
+FP8X4 = mybir.dt.float8_e4m3fn_x4
+FP4X4 = mybir.dt.float4_e2m1fn_x4
+ALU = mybir.AluOpType
+ACT = mybir.ActivationFunctionType
+
+P = 128
+D = 16384
+K_PASS = 512
+PASSES = D // K_PASS
+DH = 256
+PAIRS = DH // 2
+PAIR_BITS = 7
+assert 2**PAIR_BITS == PAIRS
+HEADS = 4
+NQ = HEADS * DH
+NKV = 2 * DH
+BANK = 512
+Q_BANKS = NQ // BANK
+ROPE_BASE = 10000.0
+EPS = 1.1920929e-07
+ROUND_MAGIC = 1.5 * 2.0**23
+
+FLOPS = 2 * P * D * (NQ + NKV)
+
+X_CHUNKS = 4
+X_CHUNK_COLS = D // X_CHUNKS
+BANK_PASSES = 2
+CHUNK_BANKS = X_CHUNK_COLS // (BANK_PASSES * K_PASS)
+
+TILE_PASSES = 2
+Q_TILES = PASSES // TILE_PASSES
+KV_TILES = PASSES // TILE_PASSES
+WORD_BUFS = 12
+AHEAD = WORD_BUFS - 1
+
+Q_BATCHES = 2
+BATCH_PASSES = PASSES // Q_BATCHES
+BATCH_TILES = Q_TILES // Q_BATCHES
+Q_SCALE_DMA_PASSES = 8
+KV_SCALE_DMA_PASSES = 16
+
+
+def load_scale_rows(nc, plane, scales_i32, first_pass, n_passes, plane_pass):
+    plane_i32 = plane[:].bitcast(I32)
+    for low in range(8):
+        part = 32 * (low // 4) + low % 4
+        nc.sync.dma_start(
+            out=plane_i32[part:P:64, plane_pass : plane_pass + n_passes, :],
+            in_=scales_i32[first_pass : first_pass + n_passes, low:16:8, :].rearrange("g q n -> q g n"),
+        )
+
+
+def tile_attention_pa_k_kernel(
+    tc, x, wq_words, wq_scales, wkv_words, wkv_scales, q_norm_w, k_norm_w, q_rot, k_rot, v_out
+):
+    nc = tc.nc
+    x_rows = x.flatten_outer_dims()
+    wq_words_i32 = wq_words.bitcast(I32)
+    wkv_words_i32 = wkv_words.bitcast(I32)
+    wq_scales_i32 = wq_scales.bitcast(I32)
+    wkv_scales_i32 = wkv_scales.bitcast(I32)
+
+    with ExitStack() as ctx:
+        ctx.enter_context(tc.manual_schedule())
+        keep = ctx.enter_context(tc.tile_pool(name="keep", bufs=1))
+        x_pool = ctx.enter_context(tc.tile_pool(name="x_pool", bufs=X_CHUNKS))
+        grouped_pool = ctx.enter_context(tc.tile_pool(name="grouped_pool", bufs=4))
+        words_pool = ctx.enter_context(tc.tile_pool(name="words_pool", bufs=WORD_BUFS))
+        work = ctx.enter_context(tc.tile_pool(name="work", bufs=2))
+        xt_pool = ctx.enter_context(tc.psum_pool(name="xt_pool", bufs=4))
+        acc_pool = ctx.enter_context(tc.psum_pool(name="acc_pool", bufs=1))
+
+        x_chunks = []
+        for c in range(X_CHUNKS):
+            x_sb = x_pool.tile([P, X_CHUNK_COLS], BF16, name="x_sb", tag="x_sb")
+            nc.sync.dma_start(out=x_sb[:], in_=x_rows[:, c * X_CHUNK_COLS : (c + 1) * X_CHUNK_COLS])
+            x_chunks.append(x_sb)
+
+        gain_rows = keep.tile([P, 2 * DH], BF16, name="gain_rows")
+        nc.gpsimd.memset(gain_rows[:], 0.0)
+        nc.scalar.dma_start(out=gain_rows[0:1, 0:DH], in_=q_norm_w.rearrange("(o d) -> o d", o=1))
+        nc.scalar.dma_start(out=gain_rows[0:1, DH : 2 * DH], in_=k_norm_w.rearrange("(o d) -> o d", o=1))
+        position_i = keep.tile([P, 1], I32, name="position_i")
+        nc.gpsimd.iota(position_i[:], pattern=[[0, 1]], base=0, channel_multiplier=1)
+        ones = keep.tile([P, P], BF16, name="ones")
+        nc.gpsimd.memset(ones[:], 1.0)
+        identity = keep.tile([P, P], F32, name="identity")
+        make_identity(nc, identity[:])
+
+        position = keep.tile([P, 1], F32, name="position")
+        nc.vector.tensor_copy(out=position[:], in_=position_i[:])
+        phase = keep.tile([P, 2, PAIRS], F32, name="phase")
+        nc.vector.tensor_scalar_mul(out=phase[:, 1, 0:1], in0=position[:], scalar1=1.0 / (2.0 * math.pi))
+        for level in range(PAIR_BITS):
+            width = 2**level
+            nc.vector.tensor_scalar_mul(
+                out=phase[:, 1, width : 2 * width],
+                in0=phase[:, 1, 0:width],
+                scalar1=ROPE_BASE ** (-2.0 * width / DH),
+            )
+        nc.vector.tensor_scalar_add(out=phase[:, 0, :], in0=phase[:, 1, :], scalar1=0.25)
+        shifted = keep.tile([P, 2, PAIRS], F32, name="shifted")
+        nc.vector.tensor_scalar_add(out=shifted[:], in0=phase[:], scalar1=ROUND_MAGIC)
+        whole = keep.tile([P, 2, PAIRS], F32, name="whole")
+        nc.vector.tensor_scalar_sub(out=whole[:], in0=shifted[:], scalar1=ROUND_MAGIC)
+        frac = keep.tile([P, 2, PAIRS], F32, name="frac")
+        nc.vector.tensor_sub(out=frac[:], in0=phase[:], in1=whole[:])
+        cos_sin = keep.tile([P, 2, PAIRS], F32, name="cos_sin")
+        nc.scalar.activation(out=cos_sin[:], in_=frac[:], func=ACT.Sin, scale=2.0 * math.pi)
+        nsin_cos = keep.tile([P, 2, PAIRS], F32, name="nsin_cos")
+        nc.scalar.activation(out=nsin_cos[:, 0, :], in_=frac[:, 1, :], func=ACT.Sin, scale=-2.0 * math.pi)
+        nc.scalar.activation(out=nsin_cos[:, 1, :], in_=frac[:, 0, :], func=ACT.Sin, scale=2.0 * math.pi)
+
+        q_planes = []
+        for b in range(Q_BATCHES):
+            q_plane = keep.tile([P, BATCH_PASSES, NQ], U8, name="q_plane%d" % b, align_bytes=64)
+            nc.vector.memset(q_plane[:].bitcast(I32), 0)
+            q_planes.append(q_plane)
+        kv_plane = keep.tile([P, PASSES, NKV], U8, name="kv_plane", align_bytes=64)
+        nc.vector.memset(kv_plane[:].bitcast(I32), 0)
+
+        gain_bank = acc_pool.tile([P, 2 * DH], F32, name="gain_bank")
+        nc.tensor.matmul(out=gain_bank[:], lhsT=ones[:], rhs=gain_rows[:], start=True, stop=True)
+
+        x_codes = keep.tile([P, PASSES * P], U32, name="x_codes", align_bytes=64)
+        x_plane = keep.tile([P, PASSES * P], U8, name="x_plane", align_bytes=64)
+        for c in range(X_CHUNKS):
+            x_words = x_chunks[c][:].bitcast(F32)
+            for b in range(CHUNK_BANKS):
+                xt = xt_pool.tile([P, BANK_PASSES, 2, P], F32, name="xt", tag="xt")
+                for a in range(BANK_PASSES):
+                    first_word = (b * BANK_PASSES + a) * (K_PASS // 2)
+                    for u in range(2):
+                        nc.tensor.transpose(
+                            xt[:, a, u, :],
+                            x_words[:, first_word + u : first_word + K_PASS // 2 : 2],
+                            identity[:],
+                        )
+                grouped = grouped_pool.tile([P, BANK_PASSES * P * 4], BF16, name="grouped", tag="grouped", align_bytes=64)
+                nc.scalar.copy(
+                    out=grouped[:].bitcast(F32).rearrange("p (a r u) -> p a r u", a=BANK_PASSES, u=2),
+                    in_=xt[:].rearrange("p a u r -> p a r u"),
+                )
+                first_col = (c * CHUNK_BANKS + b) * BANK_PASSES * P
+                cols = slice(first_col, first_col + BANK_PASSES * P)
+                nc.vector.quantize_mx(out=x_codes[:, cols].bitcast(FP8X4), scales=x_plane[:, cols], in_=grouped[:])
+
+        tables = {}
+        for which, first in (("q", 0), ("k", DH)):
+            gains = gain_bank[:, first : first + DH].rearrange("p (i e) -> p e i", e=2)
+            from_even = keep.tile([P, 2, PAIRS], F32, name="from_even_" + which)
+            nc.vector.tensor_tensor(out=from_even[:], in0=gains, in1=cos_sin[:], op=ALU.mult)
+            from_odd = keep.tile([P, 2, PAIRS], F32, name="from_odd_" + which)
+            nc.vector.tensor_tensor(out=from_odd[:], in0=gains, in1=nsin_cos[:], op=ALU.mult)
+            tables[which] = (from_even, from_odd)
+
+        squares = keep.tile([P, HEADS + 1, DH], F32, name="squares")
+
+        def mean_square_root(head, slot):
+            total = keep.tile([P, 1], F32, name="total%d" % slot)
+            nc.scalar.activation(out=squares[:, slot, :], in_=head, func=ACT.Square, accum_out=total[:])
+            rms = keep.tile([P, 1], F32, name="rms%d" % slot)
+            nc.scalar.activation(out=rms[:], in_=total[:], func=ACT.Sqrt, scale=1.0 / DH, bias=EPS)
+            return rms
+
+        def rope_even_part(head, which):
+            pairs = head.rearrange("p (i e) -> p e i", e=2)
+            part = work.tile([P, 2, PAIRS], F32, name="even_part", tag="even_part")
+            nc.vector.tensor_tensor(
+                out=part[:], in0=pairs[:, 0:1, :].to_broadcast([P, 2, PAIRS]), in1=tables[which][0][:], op=ALU.mult
+            )
+            return part
+
+        def rope_finish(head, which, even_part, rms, slot, out_head):
+            inv = keep.tile([P, 1], F32, name="inv%d" % slot)
+            nc.vector.reciprocal(out=inv[:], in_=rms[:])
+            pairs = head.rearrange("p (i e) -> p e i", e=2)
+            odd_part = work.tile([P, 2, PAIRS], F32, name="odd_part", tag="odd_part")
+            nc.vector.scalar_tensor_tensor(
+                out=odd_part[:],
+                in0=pairs[:, 1:2, :].to_broadcast([P, 2, PAIRS]),
+                scalar=inv[:],
+                in1=tables[which][1][:],
+                op0=ALU.mult,
+                op1=ALU.mult,
+            )
+            nc.vector.scalar_tensor_tensor(
+                out=out_head.rearrange("p (i e) -> p i e", e=2),
+                in0=even_part[:].rearrange("p e i -> p i e"),
+                scalar=inv[:],
+                in1=odd_part[:].rearrange("p e i -> p i e"),
+                op0=ALU.mult,
+                op1=ALU.add,
+            )
+
+        acc_q = [acc_pool.tile([P, BANK], F32, name="acc_q%d" % j) for j in range(Q_BANKS)]
+        acc_kv = acc_pool.tile([P, BANK], F32, name="acc_kv")
+        q_out = keep.tile([P, HEADS, DH], F32, name="q_out")
+        k_out = keep.tile([P, DH], F32, name="k_out")
+        v_sb = keep.tile([P, DH], F32, name="v_sb")
+
+        def load_words(s):
+            if s < Q_TILES:
+                if s % BATCH_TILES == 0:
+                    batch = s // BATCH_TILES
+                    for first in range(0, BATCH_PASSES, Q_SCALE_DMA_PASSES):
+                        load_scale_rows(
+                            nc, q_planes[batch], wq_scales_i32, batch * BATCH_PASSES + first, Q_SCALE_DMA_PASSES, first
+                        )
+                if s == Q_TILES - BATCH_TILES:
+                    for first in range(0, PASSES, KV_SCALE_DMA_PASSES):
+                        load_scale_rows(nc, kv_plane, wkv_scales_i32, first, KV_SCALE_DMA_PASSES, first)
+                first_pass = s * TILE_PASSES
+                source = wq_words_i32[first_pass : first_pass + TILE_PASSES]
+                words = words_pool.tile([P, TILE_PASSES, 2 * NQ], U8, name="words", tag="words", align_bytes=64)
+            else:
+                first_pass = (s - Q_TILES) * TILE_PASSES
+                source = wkv_words_i32[first_pass : first_pass + TILE_PASSES]
+                words = words_pool.tile([P, TILE_PASSES, 2 * NKV], U8, name="words", tag="words", align_bytes=64)
+            nc.sync.dma_start(out=words[:].bitcast(I32), in_=source.rearrange("g p w -> p g w"))
+            return words
+
+        def mx_pass(acc, g, words, scale_bytes):
+            nc.tensor.matmul_mx(
+                out=acc[:],
+                lhsT=x_codes[:, g * P : (g + 1) * P].bitcast(FP8X4),
+                lhsT_scale=x_plane[:, g * P : (g + 1) * P],
+                rhs=words.bitcast(FP4X4),
+                rhs_scale=scale_bytes,
+                start=(g == 0),
+                stop=(g == PASSES - 1),
+            )
+
+        def multiply(s, words):
+            for a in range(TILE_PASSES):
+                if s < Q_TILES:
+                    g = s * TILE_PASSES + a
+                    plane = q_planes[g // BATCH_PASSES]
+                    for j in range(Q_BANKS):
+                        mx_pass(
+                            acc_q[j],
+                            g,
+                            words[:, a, 2 * BANK * j : 2 * BANK * (j + 1)],
+                            plane[:, g % BATCH_PASSES, BANK * j : BANK * (j + 1)],
+                        )
+                else:
+                    g = (s - Q_TILES) * TILE_PASSES + a
+                    mx_pass(acc_kv, g, words[:, a, :], kv_plane[:, g, :])
+
+        def finish_queries():
+            for j in range(Q_BANKS):
+                heads = [acc_q[j][:, h * DH : (h + 1) * DH] for h in range(BANK // DH)]
+                slots = [j * (BANK // DH) + h for h in range(BANK // DH)]
+                roots = [mean_square_root(head, slot) for head, slot in zip(heads, slots)]
+                for head, slot, rms in zip(heads, slots, roots):
+                    even_part = rope_even_part(head, "q")
+                    rope_finish(head, "q", even_part, rms, slot, q_out[:, slot, :])
+
+        word_tiles = {}
+        for step in range(Q_TILES + KV_TILES + AHEAD):
+            if step < Q_TILES + KV_TILES:
+                word_tiles[step] = load_words(step)
+            s = step - AHEAD
+            if s >= 0:
+                multiply(s, word_tiles[s])
+            if s == Q_TILES - 1:
+                finish_queries()
+
+        k_head = acc_kv[:, 0:DH]
+        k_rms = mean_square_root(k_head, HEADS)
+        k_even = rope_even_part(k_head, "k")
+        nc.vector.tensor_copy(out=v_sb[:], in_=acc_kv[:, DH : 2 * DH])
+        rope_finish(k_head, "k", k_even, k_rms, HEADS, k_out[:])
+
+        nc.sync.dma_start(out=q_rot.rearrange("b h t d -> t (b h) d"), in_=q_out[:])
+        nc.sync.dma_start(out=v_out.flatten_outer_dims(), in_=v_sb[:])
+        nc.sync.dma_start(out=k_rot.flatten_outer_dims(), in_=k_out[:])

@@ -47,13 +47,13 @@ AHEAD = WORD_BUFS - 1
 Q_BATCHES = 2
 BATCH_PASSES = PASSES // Q_BATCHES
 BATCH_TILES = Q_TILES // Q_BATCHES
-Q_SCALE_DMA_PASSES = 8
-KV_SCALE_DMA_PASSES = 16
+ROW_PAIRS = 8
+LONG_PAIRS = 4
 
 
-def load_scale_rows(nc, plane, scales_i32, first_pass, n_passes, plane_pass):
+def load_scale_rows(nc, plane, scales_i32, first_pass, n_passes, plane_pass, pairs):
     plane_i32 = plane[:].bitcast(I32)
-    for low in range(8):
+    for low in pairs:
         part = 32 * (low // 4) + low % 4
         nc.sync.dma_start(
             out=plane_i32[part:P:64, plane_pass : plane_pass + n_passes, :],
@@ -212,15 +212,23 @@ def tile_attention_pa_k_kernel(
 
         def load_words(s):
             if s < Q_TILES:
+                if s == Q_TILES - BATCH_TILES:
+                    load_scale_rows(nc, kv_plane, wkv_scales_i32, 0, PASSES, 0, range(ROW_PAIRS))
                 if s % BATCH_TILES == 0:
                     batch = s // BATCH_TILES
-                    for first in range(0, BATCH_PASSES, Q_SCALE_DMA_PASSES):
+                    load_scale_rows(
+                        nc, q_planes[batch], wq_scales_i32, batch * BATCH_PASSES, BATCH_PASSES, 0, range(LONG_PAIRS)
+                    )
+                    for first in range(0, BATCH_PASSES, BATCH_PASSES // 2):
                         load_scale_rows(
-                            nc, q_planes[batch], wq_scales_i32, batch * BATCH_PASSES + first, Q_SCALE_DMA_PASSES, first
+                            nc,
+                            q_planes[batch],
+                            wq_scales_i32,
+                            batch * BATCH_PASSES + first,
+                            BATCH_PASSES // 2,
+                            first,
+                            range(LONG_PAIRS, ROW_PAIRS),
                         )
-                if s == Q_TILES - BATCH_TILES:
-                    for first in range(0, PASSES, KV_SCALE_DMA_PASSES):
-                        load_scale_rows(nc, kv_plane, wkv_scales_i32, first, KV_SCALE_DMA_PASSES, first)
                 first_pass = s * TILE_PASSES
                 source = wq_words_i32[first_pass : first_pass + TILE_PASSES]
                 words = words_pool.tile([P, TILE_PASSES, 2 * NQ], U8, name="words", tag="words", align_bytes=64)

@@ -33,6 +33,8 @@ ROUND_MAGIC = 1.5 * 2.0**23
 
 FLOPS = 2 * P * D * (NQ + NKV)
 
+DMA_ALIGN = 256
+
 X_CHUNKS = 4
 X_CHUNK_COLS = D // X_CHUNKS
 BANK_PASSES = 2
@@ -83,7 +85,7 @@ def tile_attention_pa_k_kernel(
 
         x_chunks = []
         for c in range(X_CHUNKS):
-            x_sb = x_pool.tile([P, X_CHUNK_COLS], BF16, name="x_sb", tag="x_sb")
+            x_sb = x_pool.tile([P, X_CHUNK_COLS], BF16, name="x_sb", tag="x_sb", align_bytes=DMA_ALIGN)
             nc.sync.dma_start(out=x_sb[:], in_=x_rows[:, c * X_CHUNK_COLS : (c + 1) * X_CHUNK_COLS])
             x_chunks.append(x_sb)
 
@@ -124,17 +126,17 @@ def tile_attention_pa_k_kernel(
 
         q_planes = []
         for b in range(Q_BATCHES):
-            q_plane = keep.tile([P, BATCH_PASSES, NQ], U8, name="q_plane%d" % b, align_bytes=64)
+            q_plane = keep.tile([P, BATCH_PASSES, NQ], U8, name="q_plane%d" % b, align_bytes=DMA_ALIGN)
             nc.vector.memset(q_plane[:].bitcast(I32), 0)
             q_planes.append(q_plane)
-        kv_plane = keep.tile([P, PASSES, NKV], U8, name="kv_plane", align_bytes=64)
+        kv_plane = keep.tile([P, PASSES, NKV], U8, name="kv_plane", align_bytes=DMA_ALIGN)
         nc.vector.memset(kv_plane[:].bitcast(I32), 0)
 
         gain_bank = acc_pool.tile([P, 2 * DH], F32, name="gain_bank")
         nc.tensor.matmul(out=gain_bank[:], lhsT=ones[:], rhs=gain_rows[:], start=True, stop=True)
 
-        x_codes = keep.tile([P, PASSES * P], U32, name="x_codes", align_bytes=64)
-        x_plane = keep.tile([P, PASSES * P], U8, name="x_plane", align_bytes=64)
+        x_codes = keep.tile([P, PASSES * P], U32, name="x_codes", align_bytes=DMA_ALIGN)
+        x_plane = keep.tile([P, PASSES * P], U8, name="x_plane", align_bytes=DMA_ALIGN)
         for c in range(X_CHUNKS):
             x_words = x_chunks[c][:].bitcast(F32)
             for b in range(CHUNK_BANKS):
@@ -147,7 +149,7 @@ def tile_attention_pa_k_kernel(
                             x_words[:, first_word + u : first_word + K_PASS // 2 : 2],
                             identity[:],
                         )
-                grouped = grouped_pool.tile([P, BANK_PASSES * P * 4], BF16, name="grouped", tag="grouped", align_bytes=64)
+                grouped = grouped_pool.tile([P, BANK_PASSES * P * 4], BF16, name="grouped", tag="grouped", align_bytes=DMA_ALIGN)
                 nc.scalar.copy(
                     out=grouped[:].bitcast(F32).rearrange("p (a r u) -> p a r u", a=BANK_PASSES, u=2),
                     in_=xt[:].rearrange("p a u r -> p a r u"),
@@ -206,9 +208,9 @@ def tile_attention_pa_k_kernel(
 
         acc_q = [acc_pool.tile([P, BANK], F32, name="acc_q%d" % j) for j in range(Q_BANKS)]
         acc_kv = acc_pool.tile([P, BANK], F32, name="acc_kv")
-        q_out = keep.tile([P, HEADS, DH], F32, name="q_out")
-        k_out = keep.tile([P, DH], F32, name="k_out")
-        v_sb = keep.tile([P, DH], F32, name="v_sb")
+        q_out = keep.tile([P, HEADS, DH], F32, name="q_out", align_bytes=DMA_ALIGN)
+        k_out = keep.tile([P, DH], F32, name="k_out", align_bytes=DMA_ALIGN)
+        v_sb = keep.tile([P, DH], F32, name="v_sb", align_bytes=DMA_ALIGN)
 
         def load_words(s):
             if s < Q_TILES:
@@ -231,11 +233,11 @@ def tile_attention_pa_k_kernel(
                         )
                 first_pass = s * TILE_PASSES
                 source = wq_words_i32[first_pass : first_pass + TILE_PASSES]
-                words = words_pool.tile([P, TILE_PASSES, 2 * NQ], U8, name="words", tag="words", align_bytes=64)
+                words = words_pool.tile([P, TILE_PASSES, 2 * NQ], U8, name="words", tag="words", align_bytes=DMA_ALIGN)
             else:
                 first_pass = (s - Q_TILES) * TILE_PASSES
                 source = wkv_words_i32[first_pass : first_pass + TILE_PASSES]
-                words = words_pool.tile([P, TILE_PASSES, 2 * NKV], U8, name="words", tag="words", align_bytes=64)
+                words = words_pool.tile([P, TILE_PASSES, 2 * NKV], U8, name="words", tag="words", align_bytes=DMA_ALIGN)
             nc.sync.dma_start(out=words[:].bitcast(I32), in_=source.rearrange("g p w -> p g w"))
             return words
 

@@ -50,6 +50,7 @@ Q_BATCHES = 2
 BATCH_PASSES = PASSES // Q_BATCHES
 BATCH_TILES = Q_TILES // Q_BATCHES
 ROW_PAIRS = 8
+CLOCK_KEEPERS = 14
 LONG_PAIRS = 4
 
 
@@ -214,8 +215,6 @@ def tile_attention_pa_k_kernel(
 
         def load_words(s):
             if s < Q_TILES:
-                if s == Q_TILES - BATCH_TILES:
-                    load_scale_rows(nc, kv_plane, wkv_scales_i32, 0, PASSES, 0, range(ROW_PAIRS))
                 if s % BATCH_TILES == 0:
                     batch = s // BATCH_TILES
                     load_scale_rows(
@@ -236,6 +235,11 @@ def tile_attention_pa_k_kernel(
                 words = words_pool.tile([P, TILE_PASSES, 2 * NQ], U8, name="words", tag="words", align_bytes=DMA_ALIGN)
             else:
                 first_pass = (s - Q_TILES) * TILE_PASSES
+                if first_pass == 0:
+                    for half in range(2):
+                        load_scale_rows(
+                            nc, kv_plane, wkv_scales_i32, half * BATCH_PASSES, BATCH_PASSES, half * BATCH_PASSES, range(ROW_PAIRS)
+                        )
                 source = wkv_words_i32[first_pass : first_pass + TILE_PASSES]
                 words = words_pool.tile([P, TILE_PASSES, 2 * NKV], U8, name="words", tag="words", align_bytes=DMA_ALIGN)
             nc.sync.dma_start(out=words[:].bitcast(I32), in_=source.rearrange("g p w -> p g w"))
@@ -286,6 +290,8 @@ def tile_attention_pa_k_kernel(
                 multiply(s, word_tiles[s])
             if s == Q_TILES - 1:
                 finish_queries()
+                for repeat in range(CLOCK_KEEPERS):
+                    nc.tensor.matmul(out=gain_bank[:], lhsT=ones[:], rhs=gain_rows[:], start=True, stop=True)
 
         k_head = acc_kv[:, 0:DH]
         k_rms = mean_square_root(k_head, HEADS)

@@ -42,7 +42,12 @@ CHUNK_BANKS = X_CHUNK_COLS // (BANK_PASSES * K_PASS)
 
 TILE_PASSES = 2
 Q_TILES = PASSES // TILE_PASSES
-KV_TILES = PASSES // TILE_PASSES
+SPLIT_PASSES = 12
+SPLIT_TILE_PASSES = 4
+KV_PASSES = PASSES - SPLIT_PASSES
+KV_TILES = KV_PASSES // TILE_PASSES
+SPLIT_TILES = SPLIT_PASSES // SPLIT_TILE_PASSES
+HALF = 128
 WORD_BUFS = 12
 AHEAD = WORD_BUFS - 1
 
@@ -212,65 +217,94 @@ def tile_attention_pa_k_kernel(
         q_out = keep.tile([P, HEADS, DH], F32, name="q_out", align_bytes=DMA_ALIGN)
         k_out = keep.tile([P, DH], F32, name="k_out", align_bytes=DMA_ALIGN)
         v_sb = keep.tile([P, DH], F32, name="v_sb", align_bytes=DMA_ALIGN)
+        kv_part = keep.tile([P, NKV], F32, name="kv_part")
+        k_head = keep.tile([P, DH], F32, name="k_head")
 
-        def load_words(s):
-            if s < Q_TILES:
-                if s % BATCH_TILES == 0:
-                    batch = s // BATCH_TILES
+        stream = [("q", s * TILE_PASSES, TILE_PASSES) for s in range(Q_TILES)]
+        stream += [("kv", s * TILE_PASSES, TILE_PASSES) for s in range(KV_TILES)]
+        for part in ("k", "v"):
+            stream += [(part, KV_PASSES + s * SPLIT_TILE_PASSES, SPLIT_TILE_PASSES) for s in range(SPLIT_TILES)]
+
+        row_bytes = {"q": (0, 2 * NQ), "kv": (0, 2 * NKV), "k": (0, 2 * DH), "v": (2 * DH, 4 * DH)}
+
+        def load_words(part, first_pass, n_passes):
+            if part == "q" and first_pass % BATCH_PASSES == 0:
+                plane = q_planes[first_pass // BATCH_PASSES]
+                load_scale_rows(nc, plane, wq_scales_i32, first_pass, BATCH_PASSES, 0, range(LONG_PAIRS))
+                for half in range(0, BATCH_PASSES, BATCH_PASSES // 2):
                     load_scale_rows(
-                        nc, q_planes[batch], wq_scales_i32, batch * BATCH_PASSES, BATCH_PASSES, 0, range(LONG_PAIRS)
+                        nc, plane, wq_scales_i32, first_pass + half, BATCH_PASSES // 2, half, range(LONG_PAIRS, ROW_PAIRS)
                     )
-                    for first in range(0, BATCH_PASSES, BATCH_PASSES // 2):
-                        load_scale_rows(
-                            nc,
-                            q_planes[batch],
-                            wq_scales_i32,
-                            batch * BATCH_PASSES + first,
-                            BATCH_PASSES // 2,
-                            first,
-                            range(LONG_PAIRS, ROW_PAIRS),
-                        )
-                first_pass = s * TILE_PASSES
-                source = wq_words_i32[first_pass : first_pass + TILE_PASSES]
-                words = words_pool.tile([P, TILE_PASSES, 2 * NQ], U8, name="words", tag="words", align_bytes=DMA_ALIGN)
-            else:
-                first_pass = (s - Q_TILES) * TILE_PASSES
-                if first_pass == 0:
-                    for half in range(2):
-                        load_scale_rows(
-                            nc, kv_plane, wkv_scales_i32, half * BATCH_PASSES, BATCH_PASSES, half * BATCH_PASSES, range(ROW_PAIRS)
-                        )
-                source = wkv_words_i32[first_pass : first_pass + TILE_PASSES]
-                words = words_pool.tile([P, TILE_PASSES, 2 * NKV], U8, name="words", tag="words", align_bytes=DMA_ALIGN)
-            nc.sync.dma_start(out=words[:].bitcast(I32), in_=source.rearrange("g p w -> p g w"))
+            if part == "kv" and first_pass == 0:
+                for half in range(0, PASSES, PASSES // 2):
+                    load_scale_rows(nc, kv_plane, wkv_scales_i32, half, PASSES // 2, half, range(ROW_PAIRS))
+            low, high = row_bytes[part]
+            source = wq_words_i32 if part == "q" else wkv_words_i32
+            words = words_pool.tile([P, n_passes, high - low], U8, name="words", tag="words", align_bytes=DMA_ALIGN)
+            nc.sync.dma_start(
+                out=words[:].bitcast(I32),
+                in_=source[first_pass : first_pass + n_passes, :, low // 4 : high // 4].rearrange("g p w -> p g w"),
+            )
             return words
 
-        def mx_pass(acc, g, words, scale_bytes):
+        def mx_pass(acc, g, words, scale_bytes, first_pass, last_pass):
             nc.tensor.matmul_mx(
-                out=acc[:],
+                out=acc,
                 lhsT=x_codes[:, g * P : (g + 1) * P].bitcast(FP8X4),
                 lhsT_scale=x_plane[:, g * P : (g + 1) * P],
                 rhs=words.bitcast(FP4X4),
                 rhs_scale=scale_bytes,
-                start=(g == 0),
-                stop=(g == PASSES - 1),
+                start=(g == first_pass),
+                stop=(g == last_pass),
             )
 
-        def multiply(s, words):
-            for a in range(TILE_PASSES):
-                if s < Q_TILES:
-                    g = s * TILE_PASSES + a
+        split_acc = {}
+
+        def multiply(part, first_pass, n_passes, words):
+            passes = range(first_pass, first_pass + n_passes)
+            if part == "q":
+                for a, g in enumerate(passes):
                     plane = q_planes[g // BATCH_PASSES]
                     for j in range(Q_BANKS):
                         mx_pass(
-                            acc_q[j],
+                            acc_q[j][:],
                             g,
                             words[:, a, 2 * BANK * j : 2 * BANK * (j + 1)],
                             plane[:, g % BATCH_PASSES, BANK * j : BANK * (j + 1)],
+                            0,
+                            PASSES - 1,
                         )
-                else:
-                    g = (s - Q_TILES) * TILE_PASSES + a
-                    mx_pass(acc_kv, g, words[:, a, :], kv_plane[:, g, :])
+            elif part == "kv":
+                for a, g in enumerate(passes):
+                    mx_pass(acc_kv[:], g, words[:, a, :], kv_plane[:, g, :], 0, KV_PASSES - 1)
+            else:
+                if first_pass == KV_PASSES:
+                    halves = []
+                    for h in range(DH // HALF):
+                        bank = xt_pool.tile([P, BANK_PASSES, 2, P], F32, name="xt", tag="xt")
+                        halves.append(bank[:, 0, 0, :])
+                    split_acc[part] = halves
+                first_col = 0 if part == "k" else DH
+                for h in range(DH // HALF):
+                    for a, g in enumerate(passes):
+                        mx_pass(
+                            split_acc[part][h],
+                            g,
+                            words[:, a, 2 * HALF * h : 2 * HALF * (h + 1)],
+                            kv_plane[:, g, first_col + HALF * h : first_col + HALF * (h + 1)],
+                            KV_PASSES,
+                            PASSES - 1,
+                        )
+
+        def add_parts(part, out):
+            first_col = 0 if part == "k" else DH
+            for h in range(DH // HALF):
+                nc.vector.tensor_tensor(
+                    out=out[:, HALF * h : HALF * (h + 1)],
+                    in0=split_acc[part][h],
+                    in1=kv_part[:, first_col + HALF * h : first_col + HALF * (h + 1)],
+                    op=ALU.add,
+                )
 
         def finish_queries():
             for j in range(Q_BANKS):
@@ -281,24 +315,32 @@ def tile_attention_pa_k_kernel(
                     even_part = rope_even_part(head, "q")
                     rope_finish(head, "q", even_part, rms, slot, q_out[:, slot, :])
 
+        def finish_key():
+            add_parts("k", k_head)
+            k_rms = mean_square_root(k_head[:], HEADS)
+            k_even = rope_even_part(k_head[:], "k")
+            rope_finish(k_head[:], "k", k_even, k_rms, HEADS, k_out[:])
+
         word_tiles = {}
-        for step in range(Q_TILES + KV_TILES + AHEAD):
-            if step < Q_TILES + KV_TILES:
-                word_tiles[step] = load_words(step)
+        for step in range(len(stream) + AHEAD):
+            if step < len(stream):
+                word_tiles[step] = load_words(*stream[step])
             s = step - AHEAD
             if s >= 0:
-                multiply(s, word_tiles[s])
-            if s == Q_TILES - 1:
-                finish_queries()
-                for repeat in range(CLOCK_KEEPERS):
-                    nc.tensor.matmul(out=gain_bank[:], lhsT=ones[:], rhs=gain_rows[:], start=True, stop=True)
+                part, first_pass, n_passes = stream[s]
+                multiply(part, first_pass, n_passes, word_tiles[s])
+                end_pass = first_pass + n_passes
+                if part == "q" and end_pass == PASSES:
+                    finish_queries()
+                    for repeat in range(CLOCK_KEEPERS):
+                        nc.tensor.matmul(out=gain_bank[:], lhsT=ones[:], rhs=gain_rows[:], start=True, stop=True)
+                elif part == "kv" and end_pass == KV_PASSES:
+                    nc.scalar.copy(out=kv_part[:], in_=acc_kv[:])
+                elif part == "k" and end_pass == PASSES:
+                    finish_key()
 
-        k_head = acc_kv[:, 0:DH]
-        k_rms = mean_square_root(k_head, HEADS)
-        k_even = rope_even_part(k_head, "k")
-        nc.vector.tensor_copy(out=v_sb[:], in_=acc_kv[:, DH : 2 * DH])
-        rope_finish(k_head, "k", k_even, k_rms, HEADS, k_out[:])
+        add_parts("v", v_sb)
 
         nc.sync.dma_start(out=q_rot.rearrange("b h t d -> t (b h) d"), in_=q_out[:])
-        nc.sync.dma_start(out=v_out.flatten_outer_dims(), in_=v_sb[:])
         nc.sync.dma_start(out=k_rot.flatten_outer_dims(), in_=k_out[:])
+        nc.sync.dma_start(out=v_out.flatten_outer_dims(), in_=v_sb[:])

@@ -219,6 +219,7 @@ def tile_attention_pa_k_kernel(
         v_sb = keep.tile([P, DH], F32, name="v_sb", align_bytes=DMA_ALIGN)
         kv_part = keep.tile([P, NKV], F32, name="kv_part")
         k_head = keep.tile([P, DH], F32, name="k_head")
+        k_turned = keep.tile([P, DH], F32, name="k_turned")
 
         stream = [("q", s * TILE_PASSES, TILE_PASSES) for s in range(Q_TILES)]
         stream += [("kv", s * TILE_PASSES, TILE_PASSES) for s in range(KV_TILES)]
@@ -317,9 +318,30 @@ def tile_attention_pa_k_kernel(
 
         def finish_key():
             add_parts("k", k_head)
-            k_rms = mean_square_root(k_head[:], HEADS)
-            k_even = rope_even_part(k_head[:], "k")
-            rope_finish(k_head[:], "k", k_even, k_rms, HEADS, k_out[:])
+            rms = mean_square_root(k_head[:], HEADS)
+            half_pairs = HALF // 2
+            parts = []
+            for h in range(DH // HALF):
+                pairs = k_head[:, HALF * h : HALF * (h + 1)].rearrange("p (i e) -> p e i", e=2)
+                for e in range(2):
+                    part = work.tile([P, 2, half_pairs], F32, name="key_part%d" % e, tag="key_part%d" % e)
+                    nc.vector.tensor_tensor(
+                        out=part[:],
+                        in0=pairs[:, e : e + 1, :].to_broadcast([P, 2, half_pairs]),
+                        in1=tables["k"][e][:, :, half_pairs * h : half_pairs * (h + 1)],
+                        op=ALU.mult,
+                    )
+                    parts.append(part)
+            for h in range(DH // HALF):
+                nc.vector.tensor_tensor(
+                    out=k_turned[:, HALF * h : HALF * (h + 1)].rearrange("p (i e) -> p i e", e=2),
+                    in0=parts[2 * h][:].rearrange("p e i -> p i e"),
+                    in1=parts[2 * h + 1][:].rearrange("p e i -> p i e"),
+                    op=ALU.add,
+                )
+            inv = keep.tile([P, 1], F32, name="inv%d" % HEADS)
+            nc.vector.reciprocal(out=inv[:], in_=rms[:])
+            nc.scalar.activation(out=k_out[:], in_=k_turned[:], func=ACT.Copy, scale=inv[:])
 
         word_tiles = {}
         for step in range(len(stream) + AHEAD):

@@ -54,8 +54,10 @@ AHEAD = WORD_BUFS - 1
 Q_BATCHES = 2
 BATCH_PASSES = PASSES // Q_BATCHES
 BATCH_TILES = Q_TILES // Q_BATCHES
+KV_BATCHES = 2
+KV_BATCH_PASSES = PASSES // KV_BATCHES
 ROW_PAIRS = 8
-CLOCK_KEEPERS = 14
+CLOCK_KEEPERS = 4
 LONG_PAIRS = 4
 
 
@@ -135,8 +137,11 @@ def tile_attention_pa_k_kernel(
             q_plane = keep.tile([P, BATCH_PASSES, NQ], U8, name="q_plane%d" % b, align_bytes=DMA_ALIGN)
             nc.vector.memset(q_plane[:].bitcast(I32), 0)
             q_planes.append(q_plane)
-        kv_plane = keep.tile([P, PASSES, NKV], U8, name="kv_plane", align_bytes=DMA_ALIGN)
-        nc.vector.memset(kv_plane[:].bitcast(I32), 0)
+        kv_planes = []
+        for b in range(KV_BATCHES):
+            kv_plane = keep.tile([P, KV_BATCH_PASSES, NKV], U8, name="kv_plane%d" % b, align_bytes=DMA_ALIGN)
+            nc.vector.memset(kv_plane[:].bitcast(I32), 0)
+            kv_planes.append(kv_plane)
 
         gain_bank = acc_pool.tile([P, 2 * DH], F32, name="gain_bank")
         nc.tensor.matmul(out=gain_bank[:], lhsT=ones[:], rhs=gain_rows[:], start=True, stop=True)
@@ -236,9 +241,10 @@ def tile_attention_pa_k_kernel(
                     load_scale_rows(
                         nc, plane, wq_scales_i32, first_pass + half, BATCH_PASSES // 2, half, range(LONG_PAIRS, ROW_PAIRS)
                     )
-            if part == "kv" and first_pass == 0:
-                for half in range(0, PASSES, PASSES // 2):
-                    load_scale_rows(nc, kv_plane, wkv_scales_i32, half, PASSES // 2, half, range(ROW_PAIRS))
+                if first_pass + BATCH_PASSES == PASSES:
+                    load_scale_rows(nc, kv_planes[0], wkv_scales_i32, 0, KV_BATCH_PASSES, 0, range(ROW_PAIRS))
+            if part == "kv" and first_pass == KV_BATCH_PASSES:
+                load_scale_rows(nc, kv_planes[1], wkv_scales_i32, KV_BATCH_PASSES, KV_BATCH_PASSES, 0, range(ROW_PAIRS))
             low, high = row_bytes[part]
             source = wq_words_i32 if part == "q" else wkv_words_i32
             words = words_pool.tile([P, n_passes, high - low], U8, name="words", tag="words", align_bytes=DMA_ALIGN)
@@ -259,6 +265,9 @@ def tile_attention_pa_k_kernel(
                 stop=(g == last_pass),
             )
 
+        def kv_scales(g, first_col, columns):
+            return kv_planes[g // KV_BATCH_PASSES][:, g % KV_BATCH_PASSES, first_col : first_col + columns]
+
         split_acc = {}
 
         def multiply(part, first_pass, n_passes, words):
@@ -277,7 +286,7 @@ def tile_attention_pa_k_kernel(
                         )
             elif part == "kv":
                 for a, g in enumerate(passes):
-                    mx_pass(acc_kv[:], g, words[:, a, :], kv_plane[:, g, :], 0, KV_PASSES - 1)
+                    mx_pass(acc_kv[:], g, words[:, a, :], kv_scales(g, 0, NKV), 0, KV_PASSES - 1)
             else:
                 if first_pass == KV_PASSES:
                     halves = []
@@ -292,7 +301,7 @@ def tile_attention_pa_k_kernel(
                             split_acc[part][h],
                             g,
                             words[:, a, 2 * HALF * h : 2 * HALF * (h + 1)],
-                            kv_plane[:, g, first_col + HALF * h : first_col + HALF * (h + 1)],
+                            kv_scales(g, first_col + HALF * h, HALF),
                             KV_PASSES,
                             PASSES - 1,
                         )
@@ -354,6 +363,7 @@ def tile_attention_pa_k_kernel(
                 end_pass = first_pass + n_passes
                 if part == "q" and end_pass == PASSES:
                     finish_queries()
+                elif part == "kv" and end_pass == KV_BATCH_PASSES:
                     for repeat in range(CLOCK_KEEPERS):
                         nc.tensor.matmul(out=gain_bank[:], lhsT=ones[:], rhs=gain_rows[:], start=True, stop=True)
                 elif part == "kv" and end_pass == KV_PASSES:

@@ -43,10 +43,11 @@ CHUNK_BANKS = X_CHUNK_COLS // (BANK_PASSES * K_PASS)
 TILE_PASSES = 2
 Q_TILES = PASSES // TILE_PASSES
 SPLIT_PASSES = 12
-SPLIT_TILE_PASSES = 4
+K_LOADS = (4, 4, 4)
+V_LOADS = (4, 4, 2, 2)
+assert sum(K_LOADS) == sum(V_LOADS) == SPLIT_PASSES
 KV_PASSES = PASSES - SPLIT_PASSES
 KV_TILES = KV_PASSES // TILE_PASSES
-SPLIT_TILES = SPLIT_PASSES // SPLIT_TILE_PASSES
 HALF = 128
 WORD_BUFS = 12
 AHEAD = WORD_BUFS - 1
@@ -228,8 +229,8 @@ def tile_attention_pa_k_kernel(
 
         stream = [("q", s * TILE_PASSES, TILE_PASSES) for s in range(Q_TILES)]
         stream += [("kv", s * TILE_PASSES, TILE_PASSES) for s in range(KV_TILES)]
-        for part in ("k", "v"):
-            stream += [(part, KV_PASSES + s * SPLIT_TILE_PASSES, SPLIT_TILE_PASSES) for s in range(SPLIT_TILES)]
+        for part, loads in (("k", K_LOADS), ("v", V_LOADS)):
+            stream += [(part, KV_PASSES + sum(loads[:s]), loads[s]) for s in range(len(loads))]
 
         row_bytes = {"q": (0, 2 * NQ), "kv": (0, 2 * NKV), "k": (0, 2 * DH), "v": (2 * DH, 4 * DH)}
 
@@ -351,6 +352,7 @@ def tile_attention_pa_k_kernel(
             inv = keep.tile([P, 1], F32, name="inv%d" % HEADS)
             nc.vector.reciprocal(out=inv[:], in_=rms[:])
             nc.scalar.activation(out=k_out[:], in_=k_turned[:], func=ACT.Copy, scale=inv[:])
+            nc.scalar.dma_start(out=k_rot.flatten_outer_dims(), in_=k_out[:])
 
         word_tiles = {}
         for step in range(len(stream) + AHEAD):
@@ -374,5 +376,4 @@ def tile_attention_pa_k_kernel(
         add_parts("v", v_sb)
 
         nc.sync.dma_start(out=q_rot.rearrange("b h t d -> t (b h) d"), in_=q_out[:])
-        nc.sync.dma_start(out=k_rot.flatten_outer_dims(), in_=k_out[:])
         nc.sync.dma_start(out=v_out.flatten_outer_dims(), in_=v_sb[:])

@@ -148,7 +148,7 @@ def tile_attention_pa_k_kernel(
         nc.tensor.matmul(out=gain_bank[:], lhsT=ones[:], rhs=gain_rows[:], start=True, stop=True)
 
         x_codes = keep.tile([P, PASSES * P], U32, name="x_codes", align_bytes=DMA_ALIGN)
-        x_plane = keep.tile([P, PASSES * P], U8, name="x_plane", align_bytes=DMA_ALIGN)
+        x_plane = keep.tile([P, PASSES, DMA_ALIGN], U8, name="x_plane", align_bytes=DMA_ALIGN)
         for c in range(X_CHUNKS):
             x_words = x_chunks[c][:].bitcast(F32)
             for b in range(CHUNK_BANKS):
@@ -166,9 +166,13 @@ def tile_attention_pa_k_kernel(
                     out=grouped[:].bitcast(F32).rearrange("p (a r u) -> p a r u", a=BANK_PASSES, u=2),
                     in_=xt[:].rearrange("p a u r -> p a r u"),
                 )
-                first_col = (c * CHUNK_BANKS + b) * BANK_PASSES * P
-                cols = slice(first_col, first_col + BANK_PASSES * P)
-                nc.vector.quantize_mx(out=x_codes[:, cols].bitcast(FP8X4), scales=x_plane[:, cols], in_=grouped[:])
+                for a in range(BANK_PASSES):
+                    g = (c * CHUNK_BANKS + b) * BANK_PASSES + a
+                    nc.vector.quantize_mx(
+                        out=x_codes[:, g * P : (g + 1) * P].bitcast(FP8X4),
+                        scales=x_plane[:, g, 0:P],
+                        in_=grouped[:, a * K_PASS : (a + 1) * K_PASS],
+                    )
 
         tables = {}
         for which, first in (("q", 0), ("k", DH)):
@@ -259,7 +263,7 @@ def tile_attention_pa_k_kernel(
             nc.tensor.matmul_mx(
                 out=acc,
                 lhsT=x_codes[:, g * P : (g + 1) * P].bitcast(FP8X4),
-                lhsT_scale=x_plane[:, g * P : (g + 1) * P],
+                lhsT_scale=x_plane[:, g, 0:P],
                 rhs=words.bitcast(FP4X4),
                 rhs_scale=scale_bytes,
                 start=(g == first_pass),

import math
from contextlib import ExitStack

import concourse.mybir as mybir
from concourse.masks import make_identity

F32 = mybir.dt.float32
BF16 = mybir.dt.bfloat16
I32 = mybir.dt.int32
U32 = mybir.dt.uint32
U8 = mybir.dt.uint8
FP8X4 = mybir.dt.float8_e4m3fn_x4
FP4X4 = mybir.dt.float4_e2m1fn_x4
ALU = mybir.AluOpType
ACT = mybir.ActivationFunctionType

P = 128
D = 16384
K_PASS = 512
PASSES = D // K_PASS
DH = 256
PAIRS = DH // 2
PAIR_BITS = 7
assert 2**PAIR_BITS == PAIRS
HEADS = 4
NQ = HEADS * DH
NKV = 2 * DH
BANK = 512
Q_BANKS = NQ // BANK
ROPE_BASE = 10000.0
EPS = 1.1920929e-07
ROUND_MAGIC = 1.5 * 2.0**23

FLOPS = 2 * P * D * (NQ + NKV)

DMA_ALIGN = 256

X_CHUNKS = 4
X_CHUNK_COLS = D // X_CHUNKS
BANK_PASSES = 2
CHUNK_BANKS = X_CHUNK_COLS // (BANK_PASSES * K_PASS)

TILE_PASSES = 2
Q_TILES = PASSES // TILE_PASSES
SPLIT_PASSES = 12
K_LOADS = (4, 4, 4)
V_LOADS = (4, 4, 2, 2)
assert sum(K_LOADS) == sum(V_LOADS) == SPLIT_PASSES
KV_PASSES = PASSES - SPLIT_PASSES
KV_TILES = KV_PASSES // TILE_PASSES
HALF = 128
WORD_BUFS = 12
AHEAD = WORD_BUFS - 1

Q_BATCHES = 2
BATCH_PASSES = PASSES // Q_BATCHES
BATCH_TILES = Q_TILES // Q_BATCHES
KV_BATCHES = 2
KV_BATCH_PASSES = PASSES // KV_BATCHES
ROW_PAIRS = 8
CLOCK_KEEPERS = 4
LONG_PAIRS = 4


def load_scale_rows(nc, plane, scales_i32, first_pass, n_passes, plane_pass, pairs):
    plane_i32 = plane[:].bitcast(I32)
    for low in pairs:
        part = 32 * (low // 4) + low % 4
        nc.sync.dma_start(
            out=plane_i32[part:P:64, plane_pass : plane_pass + n_passes, :],
            in_=scales_i32[first_pass : first_pass + n_passes, low:16:8, :].rearrange("g q n -> q g n"),
        )


def tile_attention_pa_k_kernel(
    tc, x, wq_words, wq_scales, wkv_words, wkv_scales, q_norm_w, k_norm_w, q_rot, k_rot, v_out
):
    nc = tc.nc
    x_rows = x.flatten_outer_dims()
    wq_words_i32 = wq_words.bitcast(I32)
    wkv_words_i32 = wkv_words.bitcast(I32)
    wq_scales_i32 = wq_scales.bitcast(I32)
    wkv_scales_i32 = wkv_scales.bitcast(I32)

    with ExitStack() as ctx:
        ctx.enter_context(tc.manual_schedule())
        keep = ctx.enter_context(tc.tile_pool(name="keep", bufs=1))
        x_pool = ctx.enter_context(tc.tile_pool(name="x_pool", bufs=X_CHUNKS))
        grouped_pool = ctx.enter_context(tc.tile_pool(name="grouped_pool", bufs=4))
        words_pool = ctx.enter_context(tc.tile_pool(name="words_pool", bufs=WORD_BUFS))
        work = ctx.enter_context(tc.tile_pool(name="work", bufs=2))
        xt_pool = ctx.enter_context(tc.psum_pool(name="xt_pool", bufs=4))
        acc_pool = ctx.enter_context(tc.psum_pool(name="acc_pool", bufs=1))

        x_chunks = []
        for c in range(X_CHUNKS):
            x_sb = x_pool.tile([P, X_CHUNK_COLS], BF16, name="x_sb", tag="x_sb", align_bytes=DMA_ALIGN)
            nc.sync.dma_start(out=x_sb[:], in_=x_rows[:, c * X_CHUNK_COLS : (c + 1) * X_CHUNK_COLS])
            x_chunks.append(x_sb)

        gain_rows = keep.tile([P, 2 * DH], BF16, name="gain_rows")
        nc.gpsimd.memset(gain_rows[:], 0.0)
        nc.scalar.dma_start(out=gain_rows[0:1, 0:DH], in_=q_norm_w.rearrange("(o d) -> o d", o=1))
        nc.scalar.dma_start(out=gain_rows[0:1, DH : 2 * DH], in_=k_norm_w.rearrange("(o d) -> o d", o=1))
        position_i = keep.tile([P, 1], I32, name="position_i")
        nc.gpsimd.iota(position_i[:], pattern=[[0, 1]], base=0, channel_multiplier=1)
        ones = keep.tile([P, P], BF16, name="ones")
        nc.gpsimd.memset(ones[:], 1.0)
        identity = keep.tile([P, P], F32, name="identity")
        make_identity(nc, identity[:])

        position = keep.tile([P, 1], F32, name="position")
        nc.vector.tensor_copy(out=position[:], in_=position_i[:])
        phase = keep.tile([P, 2, PAIRS], F32, name="phase")
        nc.vector.tensor_scalar_mul(out=phase[:, 1, 0:1], in0=position[:], scalar1=1.0 / (2.0 * math.pi))
        for level in range(PAIR_BITS):
            width = 2**level
            nc.vector.tensor_scalar_mul(
                out=phase[:, 1, width : 2 * width],
                in0=phase[:, 1, 0:width],
                scalar1=ROPE_BASE ** (-2.0 * width / DH),
            )
        nc.vector.tensor_scalar_add(out=phase[:, 0, :], in0=phase[:, 1, :], scalar1=0.25)
        shifted = keep.tile([P, 2, PAIRS], F32, name="shifted")
        nc.vector.tensor_scalar_add(out=shifted[:], in0=phase[:], scalar1=ROUND_MAGIC)
        whole = keep.tile([P, 2, PAIRS], F32, name="whole")
        nc.vector.tensor_scalar_sub(out=whole[:], in0=shifted[:], scalar1=ROUND_MAGIC)
        frac = keep.tile([P, 2, PAIRS], F32, name="frac")
        nc.vector.tensor_sub(out=frac[:], in0=phase[:], in1=whole[:])
        cos_sin = keep.tile([P, 2, PAIRS], F32, name="cos_sin")
        nc.scalar.activation(out=cos_sin[:], in_=frac[:], func=ACT.Sin, scale=2.0 * math.pi)
        nsin_cos = keep.tile([P, 2, PAIRS], F32, name="nsin_cos")
        nc.scalar.activation(out=nsin_cos[:, 0, :], in_=frac[:, 1, :], func=ACT.Sin, scale=-2.0 * math.pi)
        nc.scalar.activation(out=nsin_cos[:, 1, :], in_=frac[:, 0, :], func=ACT.Sin, scale=2.0 * math.pi)

        q_planes = []
        for b in range(Q_BATCHES):
            q_plane = keep.tile([P, BATCH_PASSES, NQ], U8, name="q_plane%d" % b, align_bytes=DMA_ALIGN)
            nc.vector.memset(q_plane[:].bitcast(I32), 0)
            q_planes.append(q_plane)
        kv_planes = []
        for b in range(KV_BATCHES):
            kv_plane = keep.tile([P, KV_BATCH_PASSES, NKV], U8, name="kv_plane%d" % b, align_bytes=DMA_ALIGN)
            nc.vector.memset(kv_plane[:].bitcast(I32), 0)
            kv_planes.append(kv_plane)

        gain_bank = acc_pool.tile([P, 2 * DH], F32, name="gain_bank")
        nc.tensor.matmul(out=gain_bank[:], lhsT=ones[:], rhs=gain_rows[:], start=True, stop=True)

        x_codes = keep.tile([P, PASSES * P], U32, name="x_codes", align_bytes=DMA_ALIGN)
        x_plane = keep.tile([P, PASSES, DMA_ALIGN], U8, name="x_plane", align_bytes=DMA_ALIGN)
        for c in range(X_CHUNKS):
            x_words = x_chunks[c][:].bitcast(F32)
            for b in range(CHUNK_BANKS):
                xt = xt_pool.tile([P, BANK_PASSES, 2, P], F32, name="xt", tag="xt")
                for a in range(BANK_PASSES):
                    first_word = (b * BANK_PASSES + a) * (K_PASS // 2)
                    for u in range(2):
                        nc.tensor.transpose(
                            xt[:, a, u, :],
                            x_words[:, first_word + u : first_word + K_PASS // 2 : 2],
                            identity[:],
                        )
                grouped = grouped_pool.tile([P, BANK_PASSES * P * 4], BF16, name="grouped", tag="grouped", align_bytes=DMA_ALIGN)
                nc.scalar.copy(
                    out=grouped[:].bitcast(F32).rearrange("p (a r u) -> p a r u", a=BANK_PASSES, u=2),
                    in_=xt[:].rearrange("p a u r -> p a r u"),
                )
                for a in range(BANK_PASSES):
                    g = (c * CHUNK_BANKS + b) * BANK_PASSES + a
                    nc.vector.quantize_mx(
                        out=x_codes[:, g * P : (g + 1) * P].bitcast(FP8X4),
                        scales=x_plane[:, g, 0:P],
                        in_=grouped[:, a * K_PASS : (a + 1) * K_PASS],
                    )

        tables = {}
        for which, first in (("q", 0), ("k", DH)):
            gains = gain_bank[:, first : first + DH].rearrange("p (i e) -> p e i", e=2)
            from_even = keep.tile([P, 2, PAIRS], F32, name="from_even_" + which)
            nc.vector.tensor_tensor(out=from_even[:], in0=gains, in1=cos_sin[:], op=ALU.mult)
            from_odd = keep.tile([P, 2, PAIRS], F32, name="from_odd_" + which)
            nc.vector.tensor_tensor(out=from_odd[:], in0=gains, in1=nsin_cos[:], op=ALU.mult)
            tables[which] = (from_even, from_odd)

        squares = keep.tile([P, HEADS + 1, DH], F32, name="squares")

        def mean_square_root(head, slot):
            total = keep.tile([P, 1], F32, name="total%d" % slot)
            nc.scalar.activation(out=squares[:, slot, :], in_=head, func=ACT.Square, accum_out=total[:])
            rms = keep.tile([P, 1], F32, name="rms%d" % slot)
            nc.scalar.activation(out=rms[:], in_=total[:], func=ACT.Sqrt, scale=1.0 / DH, bias=EPS)
            return rms

        def rope_even_part(head, which):
            pairs = head.rearrange("p (i e) -> p e i", e=2)
            part = work.tile([P, 2, PAIRS], F32, name="even_part", tag="even_part")
            nc.vector.tensor_tensor(
                out=part[:], in0=pairs[:, 0:1, :].to_broadcast([P, 2, PAIRS]), in1=tables[which][0][:], op=ALU.mult
            )
            return part

        def rope_finish(head, which, even_part, rms, slot, out_head):
            inv = keep.tile([P, 1], F32, name="inv%d" % slot)
            nc.vector.reciprocal(out=inv[:], in_=rms[:])
            pairs = head.rearrange("p (i e) -> p e i", e=2)
            odd_part = work.tile([P, 2, PAIRS], F32, name="odd_part", tag="odd_part")
            nc.vector.scalar_tensor_tensor(
                out=odd_part[:],
                in0=pairs[:, 1:2, :].to_broadcast([P, 2, PAIRS]),
                scalar=inv[:],
                in1=tables[which][1][:],
                op0=ALU.mult,
                op1=ALU.mult,
            )
            nc.vector.scalar_tensor_tensor(
                out=out_head.rearrange("p (i e) -> p i e", e=2),
                in0=even_part[:].rearrange("p e i -> p i e"),
                scalar=inv[:],
                in1=odd_part[:].rearrange("p e i -> p i e"),
                op0=ALU.mult,
                op1=ALU.add,
            )

        acc_q = [acc_pool.tile([P, BANK], F32, name="acc_q%d" % j) for j in range(Q_BANKS)]
        acc_kv = acc_pool.tile([P, BANK], F32, name="acc_kv")
        q_out = keep.tile([P, HEADS, DH], F32, name="q_out", align_bytes=DMA_ALIGN)
        k_out = keep.tile([P, DH], F32, name="k_out", align_bytes=DMA_ALIGN)
        v_sb = keep.tile([P, DH], F32, name="v_sb", align_bytes=DMA_ALIGN)
        kv_part = keep.tile([P, NKV], F32, name="kv_part")
        k_head = keep.tile([P, DH], F32, name="k_head")
        k_turned = keep.tile([P, DH], F32, name="k_turned")

        stream = [("q", s * TILE_PASSES, TILE_PASSES) for s in range(Q_TILES)]
        stream += [("kv", s * TILE_PASSES, TILE_PASSES) for s in range(KV_TILES)]
        for part, loads in (("k", K_LOADS), ("v", V_LOADS)):
            stream += [(part, KV_PASSES + sum(loads[:s]), loads[s]) for s in range(len(loads))]

        row_bytes = {"q": (0, 2 * NQ), "kv": (0, 2 * NKV), "k": (0, 2 * DH), "v": (2 * DH, 4 * DH)}

        def load_words(part, first_pass, n_passes):
            if part == "q" and first_pass % BATCH_PASSES == 0:
                plane = q_planes[first_pass // BATCH_PASSES]
                load_scale_rows(nc, plane, wq_scales_i32, first_pass, BATCH_PASSES, 0, range(LONG_PAIRS))
                for half in range(0, BATCH_PASSES, BATCH_PASSES // 2):
                    load_scale_rows(
                        nc, plane, wq_scales_i32, first_pass + half, BATCH_PASSES // 2, half, range(LONG_PAIRS, ROW_PAIRS)
                    )
                if first_pass + BATCH_PASSES == PASSES:
                    load_scale_rows(nc, kv_planes[0], wkv_scales_i32, 0, KV_BATCH_PASSES, 0, range(ROW_PAIRS))
            if part == "kv" and first_pass == KV_BATCH_PASSES:
                load_scale_rows(nc, kv_planes[1], wkv_scales_i32, KV_BATCH_PASSES, KV_BATCH_PASSES, 0, range(ROW_PAIRS))
            low, high = row_bytes[part]
            source = wq_words_i32 if part == "q" else wkv_words_i32
            words = words_pool.tile([P, n_passes, high - low], U8, name="words", tag="words", align_bytes=DMA_ALIGN)
            nc.sync.dma_start(
                out=words[:].bitcast(I32),
                in_=source[first_pass : first_pass + n_passes, :, low // 4 : high // 4].rearrange("g p w -> p g w"),
            )
            return words

        def mx_pass(acc, g, words, scale_bytes, first_pass, last_pass):
            nc.tensor.matmul_mx(
                out=acc,
                lhsT=x_codes[:, g * P : (g + 1) * P].bitcast(FP8X4),
                lhsT_scale=x_plane[:, g, 0:P],
                rhs=words.bitcast(FP4X4),
                rhs_scale=scale_bytes,
                start=(g == first_pass),
                stop=(g == last_pass),
            )

        def kv_scales(g, first_col, columns):
            return kv_planes[g // KV_BATCH_PASSES][:, g % KV_BATCH_PASSES, first_col : first_col + columns]

        split_acc = {}

        def multiply(part, first_pass, n_passes, words):
            passes = range(first_pass, first_pass + n_passes)
            if part == "q":
                for a, g in enumerate(passes):
                    plane = q_planes[g // BATCH_PASSES]
                    for j in range(Q_BANKS):
                        mx_pass(
                            acc_q[j][:],
                            g,
                            words[:, a, 2 * BANK * j : 2 * BANK * (j + 1)],
                            plane[:, g % BATCH_PASSES, BANK * j : BANK * (j + 1)],
                            0,
                            PASSES - 1,
                        )
            elif part == "kv":
                for a, g in enumerate(passes):
                    mx_pass(acc_kv[:], g, words[:, a, :], kv_scales(g, 0, NKV), 0, KV_PASSES - 1)
            else:
                if first_pass == KV_PASSES:
                    halves = []
                    for h in range(DH // HALF):
                        bank = xt_pool.tile([P, BANK_PASSES, 2, P], F32, name="xt", tag="xt")
                        halves.append(bank[:, 0, 0, :])
                    split_acc[part] = halves
                first_col = 0 if part == "k" else DH
                for h in range(DH // HALF):
                    for a, g in enumerate(passes):
                        mx_pass(
                            split_acc[part][h],
                            g,
                            words[:, a, 2 * HALF * h : 2 * HALF * (h + 1)],
                            kv_scales(g, first_col + HALF * h, HALF),
                            KV_PASSES,
                            PASSES - 1,
                        )

        def add_parts(part, out):
            first_col = 0 if part == "k" else DH
            for h in range(DH // HALF):
                nc.vector.tensor_tensor(
                    out=out[:, HALF * h : HALF * (h + 1)],
                    in0=split_acc[part][h],
                    in1=kv_part[:, first_col + HALF * h : first_col + HALF * (h + 1)],
                    op=ALU.add,
                )

        def finish_queries():
            for j in range(Q_BANKS):
                heads = [acc_q[j][:, h * DH : (h + 1) * DH] for h in range(BANK // DH)]
                slots = [j * (BANK // DH) + h for h in range(BANK // DH)]
                roots = [mean_square_root(head, slot) for head, slot in zip(heads, slots)]
                for head, slot, rms in zip(heads, slots, roots):
                    even_part = rope_even_part(head, "q")
                    rope_finish(head, "q", even_part, rms, slot, q_out[:, slot, :])

        def finish_key():
            add_parts("k", k_head)
            rms = mean_square_root(k_head[:], HEADS)
            half_pairs = HALF // 2
            parts = []
            for h in range(DH // HALF):
                pairs = k_head[:, HALF * h : HALF * (h + 1)].rearrange("p (i e) -> p e i", e=2)
                for e in range(2):
                    part = work.tile([P, 2, half_pairs], F32, name="key_part%d" % e, tag="key_part%d" % e)
                    nc.vector.tensor_tensor(
                        out=part[:],
                        in0=pairs[:, e : e + 1, :].to_broadcast([P, 2, half_pairs]),
                        in1=tables["k"][e][:, :, half_pairs * h : half_pairs * (h + 1)],
                        op=ALU.mult,
                    )
                    parts.append(part)
            for h in range(DH // HALF):
                nc.vector.tensor_tensor(
                    out=k_turned[:, HALF * h : HALF * (h + 1)].rearrange("p (i e) -> p i e", e=2),
                    in0=parts[2 * h][:].rearrange("p e i -> p i e"),
                    in1=parts[2 * h + 1][:].rearrange("p e i -> p i e"),
                    op=ALU.add,
                )
            inv = keep.tile([P, 1], F32, name="inv%d" % HEADS)
            nc.vector.reciprocal(out=inv[:], in_=rms[:])
            nc.scalar.activation(out=k_out[:], in_=k_turned[:], func=ACT.Copy, scale=inv[:])
            nc.scalar.dma_start(out=k_rot.flatten_outer_dims(), in_=k_out[:])

        word_tiles = {}
        for step in range(len(stream) + AHEAD):
            if step < len(stream):
                word_tiles[step] = load_words(*stream[step])
            s = step - AHEAD
            if s >= 0:
                part, first_pass, n_passes = stream[s]
                multiply(part, first_pass, n_passes, word_tiles[s])
                end_pass = first_pass + n_passes
                if part == "q" and end_pass == PASSES:
                    finish_queries()
                elif part == "kv" and end_pass == KV_BATCH_PASSES:
                    for repeat in range(CLOCK_KEEPERS):
                        nc.tensor.matmul(out=gain_bank[:], lhsT=ones[:], rhs=gain_rows[:], start=True, stop=True)
                elif part == "kv" and end_pass == KV_PASSES:
                    nc.scalar.copy(out=kv_part[:], in_=acc_kv[:])
                elif part == "k" and end_pass == PASSES:
                    finish_key()

        add_parts("v", v_sb)

        nc.sync.dma_start(out=q_rot.rearrange("b h t d -> t (b h) d"), in_=q_out[:])
        nc.sync.dma_start(out=v_out.flatten_outer_dims(), in_=v_sb[:])
